import numpy as np
import ml_dtypes


def mxq(x, axis, fmt="e4m3"):
    dtype, down = {"e4m3": (ml_dtypes.float8_e4m3fn, 7), "e5m2": (ml_dtypes.float8_e5m2, 14)}[fmt]
    v = np.moveaxis(np.asarray(x, np.float32).astype(ml_dtypes.bfloat16).astype(np.float64), axis, -1)
    blocks = v.reshape(v.shape[:-1] + (-1, 32))
    amax = np.abs(blocks).max(-1, keepdims=True)
    byte = np.maximum(np.where(amax > 0, np.frexp(amax)[1] - 1 + 127, 0) - down, 1)
    scale = np.exp2(byte - 127.0)
    codes = (blocks / scale).astype(np.float32).astype(dtype).astype(np.float64)
    return np.moveaxis((codes * scale).reshape(v.shape), -1, axis)


WIDE = False


def mx_kscale(k):
    if not WIDE:
        return np.ones(k)
    levels = np.array([10, -10, 5, -5, 0])
    if k % 512:
        return np.exp2(np.random.permutation(np.resize(levels, k // 32))).repeat(32)
    a = np.empty((k // 512, 16))
    for p in range(k // 512):
        a[p, :8] = np.random.permutation(np.resize(levels, 8))
        for g in range(8):
            far = levels[np.abs(levels - a[p, g]) >= 10]
            a[p, g + 8] = far[np.random.randint(len(far))]
    return np.exp2(a.ravel()).repeat(32)


BF16 = ml_dtypes.bfloat16


def bf(x):
    return np.asarray(x, np.float32).astype(BF16)


def f64(x):
    return np.asarray(x).astype(np.float64)


B, S, D, H, HD = 4, 128, 2048, 16, 128
E = H * HD
HALF = HD // 2


def rope(t, fc, fs):
    p = t.reshape(B, S, H, HALF, 2)
    tr, ti = p[..., 0], p[..., 1]
    return np.stack([tr * fc - ti * fs, tr * fs + ti * fc], axis=-1).reshape(B, S, H, HD)


def draw0():
    s = mx_kscale(D)
    return {"x": bf(np.random.standard_normal((B, S, D)) * s),
            "freq_cos": bf(np.cos(np.random.standard_normal((S, HALF)))),
            "freq_sin": bf(np.sin(np.random.standard_normal((S, HALF)))),
            "wq": bf(np.random.standard_normal((E, D)) / np.sqrt(D) / s[None, :]),
            "wk": bf(np.random.standard_normal((E, D)) / np.sqrt(D) / s[None, :])}


def core(x, freq_cos, freq_sin, wq, wk):
    xq = mxq(f64(x), 2, "e4m3")
    q = (xq @ mxq(f64(wq), 1, "e4m3").T).reshape(B, S, H, HD)
    k = (xq @ mxq(f64(wk), 1, "e4m3").T).reshape(B, S, H, HD)
    fc = f64(freq_cos)[None, :, None, :]
    fs = f64(freq_sin)[None, :, None, :]
    q_rot = rope(q, fc, fs).transpose(0, 2, 1, 3)
    k_rot = rope(k, fc, fs).transpose(0, 2, 1, 3)
    return q_rot, k_rot


def e4m3fn_bytes(y):
    return np.clip(np.asarray(y, np.float64), -448.0, 448.0).astype(np.float32).astype(ml_dtypes.float8_e4m3fn).view(np.uint8)


def e4m3fn_values(b):
    return np.asarray(b, np.uint8).view(ml_dtypes.float8_e4m3fn).astype(np.float64)


def setup_inputs():
    d = draw0()
    x0 = np.asarray(d['wq']).astype(np.float64)
    s = (np.max(np.abs(x0), axis=(0,), keepdims=True) / 448.0).astype(np.float32)
    out = {}
    for k, v in d.items():
        if k == 'wq':
            out['wq_bytes'] = e4m3fn_bytes(x0 / s.astype(np.float64))
            out['wq_scale'] = s
        else:
            out[k] = v
    return out


def reference(x, freq_cos, freq_sin, wq_bytes, wq_scale, wk):
    return core(x, freq_cos, freq_sin, e4m3fn_values(wq_bytes) * wq_scale.astype(np.float64), wk)

@@ -1,0 +1,242 @@
+from contextlib import ExitStack
+
+import concourse.mybir as mybir
+from concourse.masks import make_identity
+
+B, S, D, H, HD = 4, 128, 2048, 16, 128
+HALF = HD // 2
+FLOPS = 2 * B * S * D * 2 * H * HD
+
+F32 = mybir.dt.float32
+BF16 = mybir.dt.bfloat16
+U32 = mybir.dt.uint32
+U8 = mybir.dt.uint8
+FP8 = mybir.dt.float8_e4m3fn
+FP8X4 = mybir.dt.float8_e4m3fn_x4
+MULT = mybir.AluOpType.mult
+ADD = mybir.AluOpType.add
+ET = mybir.EngineType
+
+P = 128
+PASSES = D // 512
+GROUP = 4
+NG = 8
+
+LEAD = 3
+HEAVY = (1, 3)
+LIGHT_TAIL = 2
+LAST_ADD_V = 2
+XPOS = 2
+
+
+def tile_attention_pa_kernel(tc, x, freq_cos, freq_sin, wq_bytes, wq_scale, wk, out_0, out_1):
+    nc = tc.nc
+    with ExitStack() as ctx:
+        keep = ctx.enter_context(tc.tile_pool(name="keep", bufs=1))
+        wk_pool = ctx.enter_context(tc.tile_pool(name="wkraw", bufs=4))
+        wide_pool = ctx.enter_context(tc.tile_pool(name="wide", bufs=8))
+        g_pool = ctx.enter_context(tc.tile_pool(name="grouped", bufs=8))
+        code_pool = ctx.enter_context(tc.tile_pool(name="codes", bufs=2))
+        rope_pool = ctx.enter_context(tc.tile_pool(name="rope", bufs=4))
+        res_pool = ctx.enter_context(tc.tile_pool(name="res", bufs=5))
+        psum_t = ctx.enter_context(tc.psum_pool(name="pt", bufs=4))
+        psum_a = ctx.enter_context(tc.psum_pool(name="pa", bufs=4))
+
+        ident = keep.tile([P, P], F32, name="ident")
+        make_identity(nc, ident[:])
+        perm = keep.tile([P, P], F32, name="perm")
+        nc.vector.tensor_copy(
+            out=perm[:].rearrange("p (e j) -> p e j", e=2),
+            in_=ident[:].rearrange("p (j e) -> p e j", e=2),
+        )
+
+        def is_q(i):
+            return i % 2 == 0
+
+        wk_rows = wk.rearrange("(r p) k -> p r k", p=P)
+        wq_rows = wq_bytes.rearrange("(r p) k -> p r k", p=P)
+        raw = {}
+        x_raw = []
+        scale4 = keep.tile([P, PASSES, 4], F32, name="scale4")
+        cos_b = keep.tile([P, HALF], BF16, name="cos_b")
+        sin_b = keep.tile([P, HALF], BF16, name="sin_b")
+
+        def load_group(i):
+            n = i // 2
+            for pair in range(2):
+                r0 = GROUP * n + 2 * pair
+                if is_q(i):
+                    t = keep.tile([P, 2, D], U8, name="wq_bytes%d_%d" % (n, pair))
+                    nc.sync.dma_start(out=t[:], in_=wq_rows[:, r0 : r0 + 2, :])
+                else:
+                    t = wk_pool.tile([P, 2, D], BF16, name="wk_raw")
+                    nc.sync.dma_start(out=t[:], in_=wk_rows[:, r0 : r0 + 2, :])
+                raw[(i, pair)] = t
+
+        load_group(0)
+        nc.sync.dma_start(out=scale4[:], in_=wq_scale.rearrange("o (g p t) -> p (o g) t", p=P, t=4))
+        for b in range(B):
+            t = keep.tile([P, D], BF16, name="x_raw%d" % b)
+            nc.sync.dma_start(out=t[:], in_=x[b])
+            x_raw.append(t)
+        load_group(2)
+        load_group(1)
+        nc.sync.dma_start(out=cos_b[:], in_=freq_cos)
+        nc.sync.dma_start(out=sin_b[:], in_=freq_sin)
+        for i in range(3, NG):
+            load_group(i)
+
+        cos_t = keep.tile([P, GROUP, HALF, 2], F32, name="cos_t")
+        sin_t = keep.tile([P, GROUP, HALF, 2], F32, name="sin_t")
+
+        def tables():
+            cos_w = cos_b[:].unsqueeze(1).unsqueeze(3)
+            sin_w = sin_b[:].unsqueeze(1)
+            nc.gpsimd.tensor_copy(out=cos_t[:], in_=cos_w.to_broadcast([P, GROUP, HALF, 2]))
+            nc.gpsimd.tensor_scalar(
+                out=sin_t[:, :, :, 0], in0=sin_w.to_broadcast([P, GROUP, HALF]), scalar1=-1.0, scalar2=None, op0=MULT
+            )
+            nc.gpsimd.tensor_copy(out=sin_t[:, :, :, 1], in_=sin_w.to_broadcast([P, GROUP, HALF]))
+
+        def turn(words_of, grouped, col0, gs, rows, matrix, how):
+            tp = psum_t.tile([P, 512], F32, name="tp")
+            blocks = [(g, r) for g in gs for r in rows]
+            for u in range(2):
+                for i, (g, r) in enumerate(blocks):
+                    c = (2 * u + i) * P
+                    nc.tensor.transpose(tp[:, c : c + P], words_of(r)[:, 256 * g + u : 256 * (g + 1) : 2], matrix[:])
+            if how == "scaled":
+                factor = scale4[:, gs[0], :].rearrange("p (u e) -> p u e", u=2).unsqueeze(1)
+                nc.vector.tensor_tensor(
+                    out=grouped[:, col0 : col0 + 256, :].rearrange("p c (u e) -> p c u e", u=2),
+                    in0=tp[:].bitcast(BF16).rearrange("p (u c e) -> p c u e", u=2, e=2),
+                    in1=factor.to_broadcast([P, 256, 2, 2]),
+                    op=MULT,
+                )
+            else:
+                nc.scalar.copy(
+                    out=grouped[:].bitcast(F32)[:, col0 : col0 + 256, :],
+                    in_=tp[:].rearrange("p (u c) -> p c u", u=2),
+                )
+
+        x_codes = []
+        x_scales = []
+
+        def do_x():
+            for b in range(B):
+                gx = g_pool.tile([P, 512, 4], BF16, name="grouped", align_bytes=64)
+                words = x_raw[b][:].bitcast(F32)
+                for half in range(2):
+                    turn(lambda r: words, gx, 256 * half, [2 * half, 2 * half + 1], [0], ident, "plain")
+                xc = keep.tile([P, 512], U32, name="x_codes%d" % b, align_bytes=64)
+                xs = keep.tile([P, 512], U8, name="x_scales%d" % b, align_bytes=64)
+                nc.vector.quantize_mx(out=xc[:].bitcast(FP8X4), scales=xs[:], in_=gx[:].rearrange("p c t -> p (c t)"))
+                x_codes.append(xc)
+                x_scales.append(xs)
+
+        wide = {}
+
+        def casts(i, rows, engine):
+            if i >= NG or not is_q(i):
+                return
+            for r in rows:
+                w = wide_pool.tile([P, D], BF16, name="wide")
+                src = raw[(i, r // 2)][:, r % 2, :].bitcast(FP8)
+                if engine == "V":
+                    nc.vector.tensor_copy(out=w[:], in_=src)
+                else:
+                    nc.scalar.copy(out=w[:], in_=src)
+                wide[(i, r)] = w
+
+        grouped = {}
+
+        def thalf(th):
+            i, pair = divmod(th, 2)
+            if pair == 0:
+                for g in range(PASSES):
+                    gt = g_pool.tile([P, 512, 4], BF16, name="grouped", align_bytes=64)
+                    grouped[(i, g)] = gt
+            if is_q(i):
+                words_of = lambda r: wide[(i, 2 * pair + r)][:].bitcast(F32)
+            else:
+                words_of = lambda r: raw[(i, pair)][:, r, :].bitcast(F32)
+            for g in range(PASSES):
+                turn(words_of, grouped[(i, g)], 256 * pair, [g], [0, 1], perm, "scaled" if is_q(i) else "plain")
+
+        codes = {}
+
+        def quant(i):
+            ct = code_pool.tile([P, PASSES, 512], U32, name="codes", align_bytes=64)
+            st = code_pool.tile([P, PASSES, 512], U8, name="scales", align_bytes=64)
+            for g in range(PASSES):
+                nc.vector.quantize_mx(
+                    out=ct[:, g, :].bitcast(FP8X4),
+                    scales=st[:, g, :],
+                    in_=grouped[(i, g)][:].rearrange("p c t -> p (c t)"),
+                )
+            codes[i] = (ct, st)
+
+        accs = {}
+
+        def mhalf(mh):
+            i, beta = divmod(mh, 2)
+            ct, st = codes[i]
+            for b in (2 * beta, 2 * beta + 1):
+                acc = psum_a.tile([P, 512], F32, name="acc")
+                for g in range(PASSES):
+                    cols = slice(g * P, (g + 1) * P)
+                    nc.tensor.matmul_mx(
+                        out=acc[:],
+                        lhsT=x_codes[b][:, cols].bitcast(FP8X4),
+                        lhsT_scale=x_scales[b][:, cols],
+                        rhs=ct[:, g, :].bitcast(FP8X4),
+                        rhs_scale=st[:, g, :],
+                        start=(g == 0),
+                        stop=(g == PASSES - 1),
+                    )
+                accs[(i, b)] = acc
+
+        def rhalf(mh):
+            i, beta = divmod(mh, 2)
+            n = i // 2
+            dst = out_0 if is_q(i) else out_1
+            for b in (2 * beta, 2 * beta + 1):
+                acc_v = accs[(i, b)][:].rearrange("p (h e j) -> p h j e", h=GROUP, e=2)
+                ta = rope_pool.tile([P, GROUP, HALF, 2], F32, name="ta")
+                tb = rope_pool.tile([P, GROUP, HALF, 2], F32, name="tb")
+                res = res_pool.tile([P, GROUP, HALF, 2], F32, name="res")
+                if b in HEAVY and i < NG - LIGHT_TAIL:
+                    tsw = rope_pool.tile([P, GROUP, HALF, 2], F32, name="tsw")
+                    nc.scalar.copy(out=tsw[:], in_=acc_v[:, :, :, ::-1])
+                    nc.vector.tensor_tensor(out=ta[:], in0=acc_v, in1=cos_t[:], op=MULT)
+                    nc.gpsimd.tensor_tensor(out=tb[:], in0=tsw[:], in1=sin_t[:], op=MULT)
+                    nc.gpsimd.tensor_tensor(out=res[:], in0=ta[:], in1=tb[:], op=ADD)
+                else:
+                    nc.vector.tensor_tensor(out=ta[:], in0=acc_v, in1=cos_t[:], op=MULT)
+                    nc.vector.tensor_tensor(out=tb[:], in0=acc_v[:, :, :, ::-1], in1=sin_t[:], op=MULT)
+                    if 4 * i + b >= 4 * NG - LAST_ADD_V:
+                        nc.vector.tensor_tensor(out=res[:], in0=ta[:], in1=tb[:], op=ADD)
+                    else:
+                        nc.gpsimd.tensor_tensor(out=res[:], in0=ta[:], in1=tb[:], op=ADD)
+                nc.sync.dma_start(
+                    out=dst[b, GROUP * n : GROUP * (n + 1)].rearrange("h s f -> s h f"),
+                    in_=res[:].rearrange("p h j e -> p h (j e)"),
+                )
+
+        with tc.manual_schedule(engines={ET.PE, ET.DVE, ET.Activation, ET.Pool}):
+            tables()
+            casts(0, (0, 1, 2, 3), "V")
+            casts(2, (0, 1, 2, 3), "S")
+            for s in range(-LEAD, 2 * NG):
+                th = s + LEAD
+                if th == XPOS:
+                    do_x()
+                if th < 2 * NG and is_q(th // 2) and th // 2 >= 2:
+                    casts(th // 2 + 2, (0, 1) if th % 2 == 0 else (2, 3), "S")
+                if s >= 0:
+                    mhalf(s)
+                    rhalf(s)
+                if th < 2 * NG:
+                    thalf(th)
+                    if th % 2 == 1:
+                        quant(th // 2)

@@ -15,7 +15,6 @@ FP8 = mybir.dt.float8_e4m3fn
 FP8X4 = mybir.dt.float8_e4m3fn_x4
 MULT = mybir.AluOpType.mult
 ADD = mybir.AluOpType.add
-ET = mybir.EngineType
 
 P = 128
 PASSES = D // 512
@@ -223,20 +222,19 @@ def tile_attention_pa_kernel(tc, x, freq_cos, freq_sin, wq_bytes, wq_scale, wk, 
                     in_=res[:].rearrange("p h j e -> p h (j e)"),
                 )
 
-        with tc.manual_schedule(engines={ET.PE, ET.DVE, ET.Activation, ET.Pool}):
-            tables()
-            casts(0, (0, 1, 2, 3), "V")
-            casts(2, (0, 1, 2, 3), "S")
-            for s in range(-LEAD, 2 * NG):
-                th = s + LEAD
-                if th == XPOS:
-                    do_x()
-                if th < 2 * NG and is_q(th // 2) and th // 2 >= 2:
-                    casts(th // 2 + 2, (0, 1) if th % 2 == 0 else (2, 3), "S")
-                if s >= 0:
-                    mhalf(s)
-                    rhalf(s)
-                if th < 2 * NG:
-                    thalf(th)
-                    if th % 2 == 1:
-                        quant(th // 2)
+        tables()
+        casts(0, (0, 1, 2, 3), "V")
+        casts(2, (0, 1, 2, 3), "S")
+        for s in range(-LEAD, 2 * NG):
+            th = s + LEAD
+            if th == XPOS:
+                do_x()
+            if th < 2 * NG and is_q(th // 2) and th // 2 >= 2:
+                casts(th // 2 + 2, (0, 1) if th % 2 == 0 else (2, 3), "S")
+            if s >= 0:
+                mhalf(s)
+                rhalf(s)
+            if th < 2 * NG:
+                thalf(th)
+                if th % 2 == 1:
+                    quant(th // 2)

@@ -15,6 +15,7 @@ FP8 = mybir.dt.float8_e4m3fn
 FP8X4 = mybir.dt.float8_e4m3fn_x4
 MULT = mybir.AluOpType.mult
 ADD = mybir.AluOpType.add
+COPY = mybir.ActivationFunctionType.Copy
 
 P = 128
 PASSES = D // 512
@@ -26,6 +27,7 @@ HEAVY = (1, 3)
 LIGHT_TAIL = 2
 LAST_ADD_V = 2
 XPOS = 2
+S_BANKS = ((0, 0), (1, 0))
 
 
 def tile_attention_pa_kernel(tc, x, freq_cos, freq_sin, wq_bytes, wq_scale, wk, out_0, out_1):
@@ -104,7 +106,16 @@ def tile_attention_pa_kernel(tc, x, freq_cos, freq_sin, wq_bytes, wq_scale, wk, 
                 for i, (g, r) in enumerate(blocks):
                     c = (2 * u + i) * P
                     nc.tensor.transpose(tp[:, c : c + P], words_of(r)[:, 256 * g + u : 256 * (g + 1) : 2], matrix[:])
-            if how == "scaled":
+            if how == "scaled" and (col0 // 256, gs[0]) in S_BANKS:
+                bank = tp[:].bitcast(BF16).rearrange("p (u c e) -> p u e c", u=2, e=2)
+                for t4 in range(4):
+                    nc.scalar.activation(
+                        out=grouped[:, col0 : col0 + 256, t4],
+                        in_=bank[:, t4 // 2, t4 % 2, :],
+                        func=COPY,
+                        scale=scale4[:, gs[0], t4 : t4 + 1],
+                    )
+            elif how == "scaled":
                 factor = scale4[:, gs[0], :].rearrange("p (u e) -> p u e", u=2).unsqueeze(1)
                 nc.vector.tensor_tensor(
                     out=grouped[:, col0 : col0 + 256, :].rearrange("p c (u e) -> p c u e", u=2),

@@ -27,7 +27,7 @@ HEAVY = (1, 3)
 LIGHT_TAIL = 2
 LAST_ADD_V = 2
 XPOS = 2
-S_BANKS = ((0, 0), (1, 0))
+S_BANKS = ((0, 0, 0), (1, 0, 0), (1, 1, 0), (2, 0, 0), (3, 0, 0), (3, 1, 0))
 
 
 def tile_attention_pa_kernel(tc, x, freq_cos, freq_sin, wq_bytes, wq_scale, wk, out_0, out_1):
@@ -99,14 +99,14 @@ def tile_attention_pa_kernel(tc, x, freq_cos, freq_sin, wq_bytes, wq_scale, wk, 
             )
             nc.gpsimd.tensor_copy(out=sin_t[:, :, :, 1], in_=sin_w.to_broadcast([P, GROUP, HALF]))
 
-        def turn(words_of, grouped, col0, gs, rows, matrix, how):
+        def turn(words_of, grouped, col0, gs, rows, matrix, how, qn=0):
             tp = psum_t.tile([P, 512], F32, name="tp")
             blocks = [(g, r) for g in gs for r in rows]
             for u in range(2):
                 for i, (g, r) in enumerate(blocks):
                     c = (2 * u + i) * P
                     nc.tensor.transpose(tp[:, c : c + P], words_of(r)[:, 256 * g + u : 256 * (g + 1) : 2], matrix[:])
-            if how == "scaled" and (col0 // 256, gs[0]) in S_BANKS:
+            if how == "scaled" and (qn, col0 // 256, gs[0]) in S_BANKS:
                 bank = tp[:].bitcast(BF16).rearrange("p (u c e) -> p u e c", u=2, e=2)
                 for t4 in range(4):
                     nc.scalar.activation(
@@ -171,7 +171,7 @@ def tile_attention_pa_kernel(tc, x, freq_cos, freq_sin, wq_bytes, wq_scale, wk, 
             else:
                 words_of = lambda r: raw[(i, pair)][:, r, :].bitcast(F32)
             for g in range(PASSES):
-                turn(words_of, grouped[(i, g)], 256 * pair, [g], [0, 1], perm, "scaled" if is_q(i) else "plain")
+                turn(words_of, grouped[(i, g)], 256 * pair, [g], [0, 1], perm, "scaled" if is_q(i) else "plain", i // 2)
 
         codes = {}
 

@@ -27,6 +27,7 @@ HEAVY = (1, 3)
 LIGHT_TAIL = 2
 LAST_ADD_V = 2
 XPOS = 2
+CAST_W = 512
 S_BANKS = ((0, 0, 0), (1, 0, 0), (1, 1, 0), (2, 0, 0), (3, 0, 0), (3, 1, 0))
 
 
@@ -152,10 +153,11 @@ def tile_attention_pa_kernel(tc, x, freq_cos, freq_sin, wq_bytes, wq_scale, wk, 
             for r in rows:
                 w = wide_pool.tile([P, D], BF16, name="wide")
                 src = raw[(i, r // 2)][:, r % 2, :].bitcast(FP8)
-                if engine == "V":
-                    nc.vector.tensor_copy(out=w[:], in_=src)
-                else:
-                    nc.scalar.copy(out=w[:], in_=src)
+                for c0 in range(0, D, CAST_W):
+                    if engine == "V" and r % 2 == 0:
+                        nc.vector.tensor_copy(out=w[:, c0 : c0 + CAST_W], in_=src[:, c0 : c0 + CAST_W])
+                    else:
+                        nc.scalar.copy(out=w[:, c0 : c0 + CAST_W], in_=src[:, c0 : c0 + CAST_W])
                 wide[(i, r)] = w
 
         grouped = {}

@@ -23,12 +23,12 @@ GROUP = 4
 NG = 8
 
 LEAD = 3
-HEAVY = (1, 3)
+HEAVY = (3,)
 LIGHT_TAIL = 2
 LAST_ADD_V = 2
 XPOS = 2
 CAST_W = 512
-S_BANKS = ((0, 0, 0), (1, 0, 0), (1, 1, 0), (2, 0, 0), (3, 0, 0), (3, 1, 0))
+S_BANKS = ((0, 0, 0), (1, 0, 0), (1, 1, 0), (2, 0, 0), (2, 1, 0), (3, 0, 0), (3, 1, 0))
 
 
 def tile_attention_pa_kernel(tc, x, freq_cos, freq_sin, wq_bytes, wq_scale, wk, out_0, out_1):
@@ -41,8 +41,8 @@ def tile_attention_pa_kernel(tc, x, freq_cos, freq_sin, wq_bytes, wq_scale, wk, 
         code_pool = ctx.enter_context(tc.tile_pool(name="codes", bufs=2))
         rope_pool = ctx.enter_context(tc.tile_pool(name="rope", bufs=4))
         res_pool = ctx.enter_context(tc.tile_pool(name="res", bufs=5))
-        psum_t = ctx.enter_context(tc.psum_pool(name="pt", bufs=4))
-        psum_a = ctx.enter_context(tc.psum_pool(name="pa", bufs=4))
+        psum_t = ctx.enter_context(tc.psum_pool(name="pt", bufs=5))
+        psum_a = ctx.enter_context(tc.psum_pool(name="pa", bufs=3))
 
         ident = keep.tile([P, P], F32, name="ident")
         make_identity(nc, ident[:])
@@ -218,10 +218,10 @@ def tile_attention_pa_kernel(tc, x, freq_cos, freq_sin, wq_bytes, wq_scale, wk, 
                 tb = rope_pool.tile([P, GROUP, HALF, 2], F32, name="tb")
                 res = res_pool.tile([P, GROUP, HALF, 2], F32, name="res")
                 if b in HEAVY and i < NG - LIGHT_TAIL:
-                    tsw = rope_pool.tile([P, GROUP, HALF, 2], F32, name="tsw")
-                    nc.scalar.copy(out=tsw[:], in_=acc_v[:, :, :, ::-1])
-                    nc.vector.tensor_tensor(out=ta[:], in0=acc_v, in1=cos_t[:], op=MULT)
-                    nc.gpsimd.tensor_tensor(out=tb[:], in0=tsw[:], in1=sin_t[:], op=MULT)
+                    sums = rope_pool.tile([P, GROUP, HALF, 2], F32, name="sums")
+                    nc.scalar.copy(out=sums[:], in_=acc_v)
+                    nc.gpsimd.tensor_tensor(out=ta[:], in0=sums[:], in1=cos_t[:], op=MULT)
+                    nc.gpsimd.tensor_tensor(out=tb[:], in0=sums[:, :, :, ::-1], in1=sin_t[:], op=MULT)
                     nc.gpsimd.tensor_tensor(out=res[:], in0=ta[:], in1=tb[:], op=ADD)
                 else:
                     nc.vector.tensor_tensor(out=ta[:], in0=acc_v, in1=cos_t[:], op=MULT)

@@ -47,10 +47,6 @@ def tile_attention_pa_kernel(tc, x, freq_cos, freq_sin, wq_bytes, wq_scale, wk, 
         ident = keep.tile([P, P], F32, name="ident")
         make_identity(nc, ident[:])
         perm = keep.tile([P, P], F32, name="perm")
-        nc.vector.tensor_copy(
-            out=perm[:].rearrange("p (e j) -> p e j", e=2),
-            in_=ident[:].rearrange("p (j e) -> p e j", e=2),
-        )
 
         def is_q(i):
             return i % 2 == 0
@@ -174,6 +170,8 @@ def tile_attention_pa_kernel(tc, x, freq_cos, freq_sin, wq_bytes, wq_scale, wk, 
                 words_of = lambda r: raw[(i, pair)][:, r, :].bitcast(F32)
             for g in range(PASSES):
                 turn(words_of, grouped[(i, g)], 256 * pair, [g], [0, 1], perm, "scaled" if is_q(i) else "plain", i // 2)
+                if not is_q(i) and g % 2 == 1:
+                    casts(i + 1, (2 * pair + g // 2,), "S")
 
         codes = {}
 
@@ -236,14 +234,16 @@ def tile_attention_pa_kernel(tc, x, freq_cos, freq_sin, wq_bytes, wq_scale, wk, 
                 )
 
         tables()
-        casts(0, (0, 1, 2, 3), "V")
-        casts(2, (0, 1, 2, 3), "S")
+        with tc.manual_schedule(engines={mybir.EngineType.DVE}):
+            nc.vector.tensor_copy(
+                out=perm[:].rearrange("p (e j) -> p e j", e=2),
+                in_=ident[:].rearrange("p (j e) -> p e j", e=2),
+            )
+            casts(0, (0, 1, 2, 3), "V")
         for s in range(-LEAD, 2 * NG):
             th = s + LEAD
             if th == XPOS:
                 do_x()
-            if th < 2 * NG and is_q(th // 2) and th // 2 >= 2:
-                casts(th // 2 + 2, (0, 1) if th % 2 == 0 else (2, 3), "S")
             if s >= 0:
                 mhalf(s)
                 rhalf(s)

@@ -20,22 +20,19 @@ COPY = mybir.ActivationFunctionType.Copy
 P = 128
 PASSES = D // 512
 GROUP = 4
-NG = 8
+NQ = 4
 
-LEAD = 3
-HEAVY = (3,)
+HEAVY = ()
 LIGHT_TAIL = 2
 LAST_ADD_V = 2
-XPOS = 2
-CAST_W = 512
-S_BANKS = ((0, 0, 0), (1, 0, 0), (1, 1, 0), (2, 0, 0), (2, 1, 0), (3, 0, 0), (3, 1, 0))
+S_BANKS = ((0, 1, 1), (1, 0, 1), (1, 0, 3), (1, 1, 1), (1, 1, 3), (2, 0, 1), (2, 0, 3), (2, 1, 1), (2, 1, 3), (3, 0, 1), (3, 0, 3), (3, 1, 1), (3, 1, 3), )
 
 
 def tile_attention_pa_kernel(tc, x, freq_cos, freq_sin, wq_bytes, wq_scale, wk, out_0, out_1):
     nc = tc.nc
     with ExitStack() as ctx:
         keep = ctx.enter_context(tc.tile_pool(name="keep", bufs=1))
-        wk_pool = ctx.enter_context(tc.tile_pool(name="wkraw", bufs=4))
+        wk_pool = ctx.enter_context(tc.tile_pool(name="wkraw", bufs=6))
         wide_pool = ctx.enter_context(tc.tile_pool(name="wide", bufs=8))
         g_pool = ctx.enter_context(tc.tile_pool(name="grouped", bufs=8))
         code_pool = ctx.enter_context(tc.tile_pool(name="codes", bufs=2))
@@ -44,12 +41,10 @@ def tile_attention_pa_kernel(tc, x, freq_cos, freq_sin, wq_bytes, wq_scale, wk, 
         psum_t = ctx.enter_context(tc.psum_pool(name="pt", bufs=5))
         psum_a = ctx.enter_context(tc.psum_pool(name="pa", bufs=3))
 
+        ctx.enter_context(tc.manual_schedule(engines={mybir.EngineType.PE, mybir.EngineType.Activation, mybir.EngineType.DVE, mybir.EngineType.Pool}))
         ident = keep.tile([P, P], F32, name="ident")
         make_identity(nc, ident[:])
         perm = keep.tile([P, P], F32, name="perm")
-
-        def is_q(i):
-            return i % 2 == 0
 
         wk_rows = wk.rearrange("(r p) k -> p r k", p=P)
         wq_rows = wq_bytes.rearrange("(r p) k -> p r k", p=P)
@@ -59,30 +54,34 @@ def tile_attention_pa_kernel(tc, x, freq_cos, freq_sin, wq_bytes, wq_scale, wk, 
         cos_b = keep.tile([P, HALF], BF16, name="cos_b")
         sin_b = keep.tile([P, HALF], BF16, name="sin_b")
 
-        def load_group(i):
-            n = i // 2
+        def load_q(n):
             for pair in range(2):
                 r0 = GROUP * n + 2 * pair
-                if is_q(i):
-                    t = keep.tile([P, 2, D], U8, name="wq_bytes%d_%d" % (n, pair))
-                    nc.sync.dma_start(out=t[:], in_=wq_rows[:, r0 : r0 + 2, :])
-                else:
-                    t = wk_pool.tile([P, 2, D], BF16, name="wk_raw")
-                    nc.sync.dma_start(out=t[:], in_=wk_rows[:, r0 : r0 + 2, :])
-                raw[(i, pair)] = t
+                t = keep.tile([P, 2, D], U8, name="wq_bytes%d_%d" % (n, pair))
+                nc.sync.dma_start(out=t[:], in_=wq_rows[:, r0 : r0 + 2, :])
+                raw[("q", n, pair)] = t
 
-        load_group(0)
+        def load_k(n):
+            for pair in range(2):
+                r0 = GROUP * n + 2 * pair
+                t = wk_pool.tile([P, 2, D], BF16, name="wk_raw")
+                nc.sync.dma_start(out=t[:], in_=wk_rows[:, r0 : r0 + 2, :])
+                raw[("k", n, pair)] = t
+
+        load_q(0)
         nc.sync.dma_start(out=scale4[:], in_=wq_scale.rearrange("o (g p t) -> p (o g) t", p=P, t=4))
         for b in range(B):
             t = keep.tile([P, D], BF16, name="x_raw%d" % b)
             nc.sync.dma_start(out=t[:], in_=x[b])
             x_raw.append(t)
-        load_group(2)
-        load_group(1)
+        load_q(1)
+        load_k(0)
         nc.sync.dma_start(out=cos_b[:], in_=freq_cos)
         nc.sync.dma_start(out=sin_b[:], in_=freq_sin)
-        for i in range(3, NG):
-            load_group(i)
+        for n in range(2, NQ):
+            load_q(n)
+            load_k(n - 1)
+        load_k(NQ - 1)
 
         cos_t = keep.tile([P, GROUP, HALF, 2], F32, name="cos_t")
         sin_t = keep.tile([P, GROUP, HALF, 2], F32, name="sin_t")
@@ -96,158 +95,190 @@ def tile_attention_pa_kernel(tc, x, freq_cos, freq_sin, wq_bytes, wq_scale, wk, 
             )
             nc.gpsimd.tensor_copy(out=sin_t[:, :, :, 1], in_=sin_w.to_broadcast([P, GROUP, HALF]))
 
-        def turn(words_of, grouped, col0, gs, rows, matrix, how, qn=0):
+        def turn(blocks, matrix):
             tp = psum_t.tile([P, 512], F32, name="tp")
-            blocks = [(g, r) for g in gs for r in rows]
             for u in range(2):
-                for i, (g, r) in enumerate(blocks):
+                for i, words in enumerate(blocks):
                     c = (2 * u + i) * P
-                    nc.tensor.transpose(tp[:, c : c + P], words_of(r)[:, 256 * g + u : 256 * (g + 1) : 2], matrix[:])
-            if how == "scaled" and (qn, col0 // 256, gs[0]) in S_BANKS:
+                    nc.tensor.transpose(tp[:, c : c + P], words[:, u:256:2], matrix[:])
+            return tp
+
+        def empty_plain(tp, grouped, col0):
+            nc.scalar.copy(
+                out=grouped[:].bitcast(F32)[:, col0 : col0 + 256, :],
+                in_=tp[:].rearrange("p (u c) -> p c u", u=2),
+            )
+
+        def empty_scaled(tp, grouped, col0, n, pair, g):
+            if (n, pair, g) in S_BANKS:
                 bank = tp[:].bitcast(BF16).rearrange("p (u c e) -> p u e c", u=2, e=2)
                 for t4 in range(4):
                     nc.scalar.activation(
                         out=grouped[:, col0 : col0 + 256, t4],
                         in_=bank[:, t4 // 2, t4 % 2, :],
                         func=COPY,
-                        scale=scale4[:, gs[0], t4 : t4 + 1],
+                        scale=scale4[:, g, t4 : t4 + 1],
                     )
-            elif how == "scaled":
-                factor = scale4[:, gs[0], :].rearrange("p (u e) -> p u e", u=2).unsqueeze(1)
+            else:
+                factor = scale4[:, g, :].rearrange("p (u e) -> p u e", u=2).unsqueeze(1)
                 nc.vector.tensor_tensor(
                     out=grouped[:, col0 : col0 + 256, :].rearrange("p c (u e) -> p c u e", u=2),
                     in0=tp[:].bitcast(BF16).rearrange("p (u c e) -> p c u e", u=2, e=2),
                     in1=factor.to_broadcast([P, 256, 2, 2]),
                     op=MULT,
                 )
-            else:
-                nc.scalar.copy(
-                    out=grouped[:].bitcast(F32)[:, col0 : col0 + 256, :],
-                    in_=tp[:].rearrange("p (u c) -> p c u", u=2),
-                )
 
         x_codes = []
         x_scales = []
 
-        def do_x():
-            for b in range(B):
-                gx = g_pool.tile([P, 512, 4], BF16, name="grouped", align_bytes=64)
-                words = x_raw[b][:].bitcast(F32)
-                for half in range(2):
-                    turn(lambda r: words, gx, 256 * half, [2 * half, 2 * half + 1], [0], ident, "plain")
-                xc = keep.tile([P, 512], U32, name="x_codes%d" % b, align_bytes=64)
-                xs = keep.tile([P, 512], U8, name="x_scales%d" % b, align_bytes=64)
-                nc.vector.quantize_mx(out=xc[:].bitcast(FP8X4), scales=xs[:], in_=gx[:].rearrange("p c t -> p (c t)"))
-                x_codes.append(xc)
-                x_scales.append(xs)
+        def do_x(b):
+            gx = g_pool.tile([P, 512, 4], BF16, name="grouped", align_bytes=64)
+            words = x_raw[b][:].bitcast(F32)
+            for half in range(2):
+                tp = turn([words[:, 256 * g : 256 * (g + 1)] for g in (2 * half, 2 * half + 1)], ident)
+                empty_plain(tp, gx, 256 * half)
+            xc = keep.tile([P, 512], U32, name="x_codes%d" % b, align_bytes=64)
+            xs = keep.tile([P, 512], U8, name="x_scales%d" % b, align_bytes=64)
+            nc.vector.quantize_mx(out=xc[:].bitcast(FP8X4), scales=xs[:], in_=gx[:].rearrange("p c t -> p (c t)"))
+            x_codes.append(xc)
+            x_scales.append(xs)
 
         wide = {}
 
-        def casts(i, rows, engine):
-            if i >= NG or not is_q(i):
-                return
-            for r in rows:
+        def cast(n, r, engine):
+            w = wide_pool.tile([P, D], BF16, name="wide")
+            for g in range(PASSES):
+                wide[(n, r)] = w
+                cast_piece(n, r, g, engine)
+
+        def cast_piece(n, r, g, engine):
+            if g == 0 and (n, r) not in wide:
                 w = wide_pool.tile([P, D], BF16, name="wide")
-                src = raw[(i, r // 2)][:, r % 2, :].bitcast(FP8)
-                for c0 in range(0, D, CAST_W):
-                    if engine == "V" and r % 2 == 0:
-                        nc.vector.tensor_copy(out=w[:, c0 : c0 + CAST_W], in_=src[:, c0 : c0 + CAST_W])
-                    else:
-                        nc.scalar.copy(out=w[:, c0 : c0 + CAST_W], in_=src[:, c0 : c0 + CAST_W])
-                wide[(i, r)] = w
+                wide[(n, r)] = w
+            src = raw[("q", n, r // 2)][:, r % 2, 512 * g : 512 * (g + 1)].bitcast(FP8)
+            dst = wide[(n, r)][:, 512 * g : 512 * (g + 1)]
+            if engine == "V":
+                nc.vector.tensor_copy(out=dst, in_=src)
+            else:
+                nc.scalar.copy(out=dst, in_=src)
 
         grouped = {}
 
-        def thalf(th):
-            i, pair = divmod(th, 2)
+        def bank(kind, n, pair, g):
             if pair == 0:
-                for g in range(PASSES):
-                    gt = g_pool.tile([P, 512, 4], BF16, name="grouped", align_bytes=64)
-                    grouped[(i, g)] = gt
-            if is_q(i):
-                words_of = lambda r: wide[(i, 2 * pair + r)][:].bitcast(F32)
+                gt = g_pool.tile([P, 512, 4], BF16, name="grouped", align_bytes=64)
+                grouped[(kind, n, g)] = gt
+            gt = grouped[(kind, n, g)]
+            if kind == "q":
+                blocks = [wide[(n, 2 * pair + r)][:, 512 * g : 512 * (g + 1)].bitcast(F32) for r in range(2)]
+                empty_scaled(turn(blocks, perm), gt, 256 * pair, n, pair, g)
             else:
-                words_of = lambda r: raw[(i, pair)][:, r, :].bitcast(F32)
-            for g in range(PASSES):
-                turn(words_of, grouped[(i, g)], 256 * pair, [g], [0, 1], perm, "scaled" if is_q(i) else "plain", i // 2)
-                if not is_q(i) and g % 2 == 1:
-                    casts(i + 1, (2 * pair + g // 2,), "S")
+                rows = raw[("k", n, pair)]
+                blocks = [rows[:, r, 512 * g : 512 * (g + 1)].bitcast(F32) for r in range(2)]
+                empty_plain(turn(blocks, perm), gt, 256 * pair)
 
         codes = {}
 
-        def quant(i):
-            ct = code_pool.tile([P, PASSES, 512], U32, name="codes", align_bytes=64)
-            st = code_pool.tile([P, PASSES, 512], U8, name="scales", align_bytes=64)
-            for g in range(PASSES):
-                nc.vector.quantize_mx(
-                    out=ct[:, g, :].bitcast(FP8X4),
-                    scales=st[:, g, :],
-                    in_=grouped[(i, g)][:].rearrange("p c t -> p (c t)"),
-                )
-            codes[i] = (ct, st)
+        def quant(kind, n, g):
+            if g == 0:
+                ct = code_pool.tile([P, PASSES, 512], U32, name="codes", align_bytes=64)
+                st = code_pool.tile([P, PASSES, 512], U8, name="scales", align_bytes=64)
+                codes[(kind, n)] = (ct, st)
+            ct, st = codes[(kind, n)]
+            nc.vector.quantize_mx(
+                out=ct[:, g, :].bitcast(FP8X4),
+                scales=st[:, g, :],
+                in_=grouped[(kind, n, g)][:].rearrange("p c t -> p (c t)"),
+            )
 
         accs = {}
 
-        def mhalf(mh):
-            i, beta = divmod(mh, 2)
-            ct, st = codes[i]
-            for b in (2 * beta, 2 * beta + 1):
-                acc = psum_a.tile([P, 512], F32, name="acc")
-                for g in range(PASSES):
-                    cols = slice(g * P, (g + 1) * P)
-                    nc.tensor.matmul_mx(
-                        out=acc[:],
-                        lhsT=x_codes[b][:, cols].bitcast(FP8X4),
-                        lhsT_scale=x_scales[b][:, cols],
-                        rhs=ct[:, g, :].bitcast(FP8X4),
-                        rhs_scale=st[:, g, :],
-                        start=(g == 0),
-                        stop=(g == PASSES - 1),
-                    )
-                accs[(i, b)] = acc
-
-        def rhalf(mh):
-            i, beta = divmod(mh, 2)
-            n = i // 2
-            dst = out_0 if is_q(i) else out_1
-            for b in (2 * beta, 2 * beta + 1):
-                acc_v = accs[(i, b)][:].rearrange("p (h e j) -> p h j e", h=GROUP, e=2)
-                ta = rope_pool.tile([P, GROUP, HALF, 2], F32, name="ta")
-                tb = rope_pool.tile([P, GROUP, HALF, 2], F32, name="tb")
-                res = res_pool.tile([P, GROUP, HALF, 2], F32, name="res")
-                if b in HEAVY and i < NG - LIGHT_TAIL:
-                    sums = rope_pool.tile([P, GROUP, HALF, 2], F32, name="sums")
-                    nc.scalar.copy(out=sums[:], in_=acc_v)
-                    nc.gpsimd.tensor_tensor(out=ta[:], in0=sums[:], in1=cos_t[:], op=MULT)
-                    nc.gpsimd.tensor_tensor(out=tb[:], in0=sums[:, :, :, ::-1], in1=sin_t[:], op=MULT)
-                    nc.gpsimd.tensor_tensor(out=res[:], in0=ta[:], in1=tb[:], op=ADD)
-                else:
-                    nc.vector.tensor_tensor(out=ta[:], in0=acc_v, in1=cos_t[:], op=MULT)
-                    nc.vector.tensor_tensor(out=tb[:], in0=acc_v[:, :, :, ::-1], in1=sin_t[:], op=MULT)
-                    if 4 * i + b >= 4 * NG - LAST_ADD_V:
-                        nc.vector.tensor_tensor(out=res[:], in0=ta[:], in1=tb[:], op=ADD)
-                    else:
-                        nc.gpsimd.tensor_tensor(out=res[:], in0=ta[:], in1=tb[:], op=ADD)
-                nc.sync.dma_start(
-                    out=dst[b, GROUP * n : GROUP * (n + 1)].rearrange("h s f -> s h f"),
-                    in_=res[:].rearrange("p h j e -> p h (j e)"),
+        def multiply(kind, n, b):
+            ct, st = codes[(kind, n)]
+            acc = psum_a.tile([P, 512], F32, name="acc")
+            for g in range(PASSES):
+                cols = slice(g * P, (g + 1) * P)
+                nc.tensor.matmul_mx(
+                    out=acc[:],
+                    lhsT=x_codes[b][:, cols].bitcast(FP8X4),
+                    lhsT_scale=x_scales[b][:, cols],
+                    rhs=ct[:, g, :].bitcast(FP8X4),
+                    rhs_scale=st[:, g, :],
+                    start=(g == 0),
+                    stop=(g == PASSES - 1),
                 )
+            accs[(kind, n, b)] = acc
 
-        tables()
-        with tc.manual_schedule(engines={mybir.EngineType.DVE}):
-            nc.vector.tensor_copy(
-                out=perm[:].rearrange("p (e j) -> p e j", e=2),
-                in_=ident[:].rearrange("p (j e) -> p e j", e=2),
+        def rope(kind, n, b):
+            place = 8 * n + 4 * (kind == "k") + b
+            dst = out_0 if kind == "q" else out_1
+            acc_v = accs[(kind, n, b)][:].rearrange("p (h e j) -> p h j e", h=GROUP, e=2)
+            ta = rope_pool.tile([P, GROUP, HALF, 2], F32, name="ta")
+            tb = rope_pool.tile([P, GROUP, HALF, 2], F32, name="tb")
+            res = res_pool.tile([P, GROUP, HALF, 2], F32, name="res")
+            if b in HEAVY and place < 4 * (2 * NQ - LIGHT_TAIL):
+                sums = rope_pool.tile([P, GROUP, HALF, 2], F32, name="sums")
+                nc.scalar.copy(out=sums[:], in_=acc_v)
+                nc.gpsimd.tensor_tensor(out=ta[:], in0=sums[:], in1=cos_t[:], op=MULT)
+                nc.gpsimd.tensor_tensor(out=tb[:], in0=sums[:, :, :, ::-1], in1=sin_t[:], op=MULT)
+                nc.gpsimd.tensor_tensor(out=res[:], in0=ta[:], in1=tb[:], op=ADD)
+            else:
+                nc.vector.tensor_tensor(out=ta[:], in0=acc_v, in1=cos_t[:], op=MULT)
+                nc.vector.tensor_tensor(out=tb[:], in0=acc_v[:, :, :, ::-1], in1=sin_t[:], op=MULT)
+                if place >= 8 * NQ - LAST_ADD_V:
+                    nc.vector.tensor_tensor(out=res[:], in0=ta[:], in1=tb[:], op=ADD)
+                else:
+                    nc.gpsimd.tensor_tensor(out=res[:], in0=ta[:], in1=tb[:], op=ADD)
+            nc.sync.dma_start(
+                out=dst[b, GROUP * n : GROUP * (n + 1)].rearrange("h s f -> s h f"),
+                in_=res[:].rearrange("p h j e -> p h (j e)"),
             )
-            casts(0, (0, 1, 2, 3), "V")
-        for s in range(-LEAD, 2 * NG):
-            th = s + LEAD
-            if th == XPOS:
-                do_x()
-            if s >= 0:
-                mhalf(s)
-                rhalf(s)
-            if th < 2 * NG:
-                thalf(th)
-                if th % 2 == 1:
-                    quant(th // 2)
+
+        kinds = [(kind, n) for n in range(NQ) for kind in ("q", "k")]
+        units = [(kind, n, b) for kind, n in kinds for b in range(B)]
+        tables()
+        nc.vector.tensor_copy(
+            out=perm[:].rearrange("p (e j) -> p e j", e=2),
+            in_=ident[:].rearrange("p (j e) -> p e j", e=2),
+        )
+        for pair in range(2):
+            for g in range(PASSES):
+                for r in (2 * pair, 2 * pair + 1):
+                    cast_piece(0, r, g, "V" if r in (0, 2) else "S")
+        pending = []
+        late = []
+
+        def turn_bank(th, g):
+            kind, n = kinds[th // 2]
+            bank(kind, n, th % 2, g)
+            if kind == "k" and n + 1 < NQ:
+                for i in range(2):
+                    j = 2 * (4 * (th % 2) + g) + i
+                    if j < 16:
+                        cast_piece(n + 1, 2 * (j // 8) + j % 2, (j % 8) // 2, "S")
+
+        for s in range(-3, 4 * NQ):
+            th = s + 3
+            if th == 2:
+                for b in range(B):
+                    do_x(b)
+            for part in range(2):
+                if s >= 0:
+                    unit = units[2 * s + part]
+                    multiply(*unit)
+                    late.append(unit)
+
+                if th < 4 * NQ:
+                    for g in (2 * part, 2 * part + 1):
+                        turn_bank(th, g)
+                while late:
+                    rope(*late.pop(0))
+                for i in range(2):
+                    if pending:
+                        quant(*pending.pop(0))
+            if th < 4 * NQ and th % 2 == 1:
+                pending.extend([kinds[th // 2] + (g,) for g in range(PASSES)])
+                while pending:
+                    quant(*pending.pop(0))
+        for unit in late:
+            rope(*unit)

@@ -24,8 +24,8 @@ NQ = 4
 
 HEAVY = ()
 LIGHT_TAIL = 2
-LAST_ADD_V = 2
-S_BANKS = ((0, 1, 1), (1, 0, 1), (1, 0, 3), (1, 1, 1), (1, 1, 3), (2, 0, 1), (2, 0, 3), (2, 1, 1), (2, 1, 3), (3, 0, 1), (3, 0, 3), (3, 1, 1), (3, 1, 3), )
+LAST_ADD_V = 4
+S_BANKS = ((0, 1, 1), (1, 0, 1), (1, 0, 3), (1, 1, 2), (2, 0, 1), (2, 0, 3), (2, 1, 2), (3, 0, 1), (3, 0, 3), (3, 1, 2), )
 
 
 def tile_attention_pa_kernel(tc, x, freq_cos, freq_sin, wq_bytes, wq_scale, wk, out_0, out_1):
@@ -244,7 +244,7 @@ def tile_attention_pa_kernel(tc, x, freq_cos, freq_sin, wq_bytes, wq_scale, wk, 
         for pair in range(2):
             for g in range(PASSES):
                 for r in (2 * pair, 2 * pair + 1):
-                    cast_piece(0, r, g, "V" if r in (0, 2) else "S")
+                    cast_piece(0, r, g, "V" if r in (0,) else "S")
         pending = []
         late = []
 

from contextlib import ExitStack

import concourse.mybir as mybir
from concourse.masks import make_identity

B, S, D, H, HD = 4, 128, 2048, 16, 128
HALF = HD // 2
FLOPS = 2 * B * S * D * 2 * H * HD

F32 = mybir.dt.float32
BF16 = mybir.dt.bfloat16
U32 = mybir.dt.uint32
U8 = mybir.dt.uint8
FP8 = mybir.dt.float8_e4m3fn
FP8X4 = mybir.dt.float8_e4m3fn_x4
MULT = mybir.AluOpType.mult
ADD = mybir.AluOpType.add
COPY = mybir.ActivationFunctionType.Copy

P = 128
PASSES = D // 512
GROUP = 4
NQ = 4

HEAVY = ()
LIGHT_TAIL = 2
LAST_ADD_V = 4
S_BANKS = ((0, 1, 1), (1, 0, 1), (1, 0, 3), (1, 1, 2), (2, 0, 1), (2, 0, 3), (2, 1, 2), (3, 0, 1), (3, 0, 3), (3, 1, 2), )


def tile_attention_pa_kernel(tc, x, freq_cos, freq_sin, wq_bytes, wq_scale, wk, out_0, out_1):
    nc = tc.nc
    with ExitStack() as ctx:
        keep = ctx.enter_context(tc.tile_pool(name="keep", bufs=1))
        wk_pool = ctx.enter_context(tc.tile_pool(name="wkraw", bufs=6))
        wide_pool = ctx.enter_context(tc.tile_pool(name="wide", bufs=8))
        g_pool = ctx.enter_context(tc.tile_pool(name="grouped", bufs=8))
        code_pool = ctx.enter_context(tc.tile_pool(name="codes", bufs=2))
        rope_pool = ctx.enter_context(tc.tile_pool(name="rope", bufs=4))
        res_pool = ctx.enter_context(tc.tile_pool(name="res", bufs=5))
        psum_t = ctx.enter_context(tc.psum_pool(name="pt", bufs=5))
        psum_a = ctx.enter_context(tc.psum_pool(name="pa", bufs=3))

        ctx.enter_context(tc.manual_schedule(engines={mybir.EngineType.PE, mybir.EngineType.Activation, mybir.EngineType.DVE, mybir.EngineType.Pool}))
        ident = keep.tile([P, P], F32, name="ident")
        make_identity(nc, ident[:])
        perm = keep.tile([P, P], F32, name="perm")

        wk_rows = wk.rearrange("(r p) k -> p r k", p=P)
        wq_rows = wq_bytes.rearrange("(r p) k -> p r k", p=P)
        raw = {}
        x_raw = []
        scale4 = keep.tile([P, PASSES, 4], F32, name="scale4")
        cos_b = keep.tile([P, HALF], BF16, name="cos_b")
        sin_b = keep.tile([P, HALF], BF16, name="sin_b")

        def load_q(n):
            for pair in range(2):
                r0 = GROUP * n + 2 * pair
                t = keep.tile([P, 2, D], U8, name="wq_bytes%d_%d" % (n, pair))
                nc.sync.dma_start(out=t[:], in_=wq_rows[:, r0 : r0 + 2, :])
                raw[("q", n, pair)] = t

        def load_k(n):
            for pair in range(2):
                r0 = GROUP * n + 2 * pair
                t = wk_pool.tile([P, 2, D], BF16, name="wk_raw")
                nc.sync.dma_start(out=t[:], in_=wk_rows[:, r0 : r0 + 2, :])
                raw[("k", n, pair)] = t

        load_q(0)
        nc.sync.dma_start(out=scale4[:], in_=wq_scale.rearrange("o (g p t) -> p (o g) t", p=P, t=4))
        for b in range(B):
            t = keep.tile([P, D], BF16, name="x_raw%d" % b)
            nc.sync.dma_start(out=t[:], in_=x[b])
            x_raw.append(t)
        load_q(1)
        load_k(0)
        nc.sync.dma_start(out=cos_b[:], in_=freq_cos)
        nc.sync.dma_start(out=sin_b[:], in_=freq_sin)
        for n in range(2, NQ):
            load_q(n)
            load_k(n - 1)
        load_k(NQ - 1)

        cos_t = keep.tile([P, GROUP, HALF, 2], F32, name="cos_t")
        sin_t = keep.tile([P, GROUP, HALF, 2], F32, name="sin_t")

        def tables():
            cos_w = cos_b[:].unsqueeze(1).unsqueeze(3)
            sin_w = sin_b[:].unsqueeze(1)
            nc.gpsimd.tensor_copy(out=cos_t[:], in_=cos_w.to_broadcast([P, GROUP, HALF, 2]))
            nc.gpsimd.tensor_scalar(
                out=sin_t[:, :, :, 0], in0=sin_w.to_broadcast([P, GROUP, HALF]), scalar1=-1.0, scalar2=None, op0=MULT
            )
            nc.gpsimd.tensor_copy(out=sin_t[:, :, :, 1], in_=sin_w.to_broadcast([P, GROUP, HALF]))

        def turn(blocks, matrix):
            tp = psum_t.tile([P, 512], F32, name="tp")
            for u in range(2):
                for i, words in enumerate(blocks):
                    c = (2 * u + i) * P
                    nc.tensor.transpose(tp[:, c : c + P], words[:, u:256:2], matrix[:])
            return tp

        def empty_plain(tp, grouped, col0):
            nc.scalar.copy(
                out=grouped[:].bitcast(F32)[:, col0 : col0 + 256, :],
                in_=tp[:].rearrange("p (u c) -> p c u", u=2),
            )

        def empty_scaled(tp, grouped, col0, n, pair, g):
            if (n, pair, g) in S_BANKS:
                bank = tp[:].bitcast(BF16).rearrange("p (u c e) -> p u e c", u=2, e=2)
                for t4 in range(4):
                    nc.scalar.activation(
                        out=grouped[:, col0 : col0 + 256, t4],
                        in_=bank[:, t4 // 2, t4 % 2, :],
                        func=COPY,
                        scale=scale4[:, g, t4 : t4 + 1],
                    )
            else:
                factor = scale4[:, g, :].rearrange("p (u e) -> p u e", u=2).unsqueeze(1)
                nc.vector.tensor_tensor(
                    out=grouped[:, col0 : col0 + 256, :].rearrange("p c (u e) -> p c u e", u=2),
                    in0=tp[:].bitcast(BF16).rearrange("p (u c e) -> p c u e", u=2, e=2),
                    in1=factor.to_broadcast([P, 256, 2, 2]),
                    op=MULT,
                )

        x_codes = []
        x_scales = []

        def do_x(b):
            gx = g_pool.tile([P, 512, 4], BF16, name="grouped", align_bytes=64)
            words = x_raw[b][:].bitcast(F32)
            for half in range(2):
                tp = turn([words[:, 256 * g : 256 * (g + 1)] for g in (2 * half, 2 * half + 1)], ident)
                empty_plain(tp, gx, 256 * half)
            xc = keep.tile([P, 512], U32, name="x_codes%d" % b, align_bytes=64)
            xs = keep.tile([P, 512], U8, name="x_scales%d" % b, align_bytes=64)
            nc.vector.quantize_mx(out=xc[:].bitcast(FP8X4), scales=xs[:], in_=gx[:].rearrange("p c t -> p (c t)"))
            x_codes.append(xc)
            x_scales.append(xs)

        wide = {}

        def cast(n, r, engine):
            w = wide_pool.tile([P, D], BF16, name="wide")
            for g in range(PASSES):
                wide[(n, r)] = w
                cast_piece(n, r, g, engine)

        def cast_piece(n, r, g, engine):
            if g == 0 and (n, r) not in wide:
                w = wide_pool.tile([P, D], BF16, name="wide")
                wide[(n, r)] = w
            src = raw[("q", n, r // 2)][:, r % 2, 512 * g : 512 * (g + 1)].bitcast(FP8)
            dst = wide[(n, r)][:, 512 * g : 512 * (g + 1)]
            if engine == "V":
                nc.vector.tensor_copy(out=dst, in_=src)
            else:
                nc.scalar.copy(out=dst, in_=src)

        grouped = {}

        def bank(kind, n, pair, g):
            if pair == 0:
                gt = g_pool.tile([P, 512, 4], BF16, name="grouped", align_bytes=64)
                grouped[(kind, n, g)] = gt
            gt = grouped[(kind, n, g)]
            if kind == "q":
                blocks = [wide[(n, 2 * pair + r)][:, 512 * g : 512 * (g + 1)].bitcast(F32) for r in range(2)]
                empty_scaled(turn(blocks, perm), gt, 256 * pair, n, pair, g)
            else:
                rows = raw[("k", n, pair)]
                blocks = [rows[:, r, 512 * g : 512 * (g + 1)].bitcast(F32) for r in range(2)]
                empty_plain(turn(blocks, perm), gt, 256 * pair)

        codes = {}

        def quant(kind, n, g):
            if g == 0:
                ct = code_pool.tile([P, PASSES, 512], U32, name="codes", align_bytes=64)
                st = code_pool.tile([P, PASSES, 512], U8, name="scales", align_bytes=64)
                codes[(kind, n)] = (ct, st)
            ct, st = codes[(kind, n)]
            nc.vector.quantize_mx(
                out=ct[:, g, :].bitcast(FP8X4),
                scales=st[:, g, :],
                in_=grouped[(kind, n, g)][:].rearrange("p c t -> p (c t)"),
            )

        accs = {}

        def multiply(kind, n, b):
            ct, st = codes[(kind, n)]
            acc = psum_a.tile([P, 512], F32, name="acc")
            for g in range(PASSES):
                cols = slice(g * P, (g + 1) * P)
                nc.tensor.matmul_mx(
                    out=acc[:],
                    lhsT=x_codes[b][:, cols].bitcast(FP8X4),
                    lhsT_scale=x_scales[b][:, cols],
                    rhs=ct[:, g, :].bitcast(FP8X4),
                    rhs_scale=st[:, g, :],
                    start=(g == 0),
                    stop=(g == PASSES - 1),
                )
            accs[(kind, n, b)] = acc

        def rope(kind, n, b):
            place = 8 * n + 4 * (kind == "k") + b
            dst = out_0 if kind == "q" else out_1
            acc_v = accs[(kind, n, b)][:].rearrange("p (h e j) -> p h j e", h=GROUP, e=2)
            ta = rope_pool.tile([P, GROUP, HALF, 2], F32, name="ta")
            tb = rope_pool.tile([P, GROUP, HALF, 2], F32, name="tb")
            res = res_pool.tile([P, GROUP, HALF, 2], F32, name="res")
            if b in HEAVY and place < 4 * (2 * NQ - LIGHT_TAIL):
                sums = rope_pool.tile([P, GROUP, HALF, 2], F32, name="sums")
                nc.scalar.copy(out=sums[:], in_=acc_v)
                nc.gpsimd.tensor_tensor(out=ta[:], in0=sums[:], in1=cos_t[:], op=MULT)
                nc.gpsimd.tensor_tensor(out=tb[:], in0=sums[:, :, :, ::-1], in1=sin_t[:], op=MULT)
                nc.gpsimd.tensor_tensor(out=res[:], in0=ta[:], in1=tb[:], op=ADD)
            else:
                nc.vector.tensor_tensor(out=ta[:], in0=acc_v, in1=cos_t[:], op=MULT)
                nc.vector.tensor_tensor(out=tb[:], in0=acc_v[:, :, :, ::-1], in1=sin_t[:], op=MULT)
                if place >= 8 * NQ - LAST_ADD_V:
                    nc.vector.tensor_tensor(out=res[:], in0=ta[:], in1=tb[:], op=ADD)
                else:
                    nc.gpsimd.tensor_tensor(out=res[:], in0=ta[:], in1=tb[:], op=ADD)
            nc.sync.dma_start(
                out=dst[b, GROUP * n : GROUP * (n + 1)].rearrange("h s f -> s h f"),
                in_=res[:].rearrange("p h j e -> p h (j e)"),
            )

        kinds = [(kind, n) for n in range(NQ) for kind in ("q", "k")]
        units = [(kind, n, b) for kind, n in kinds for b in range(B)]
        tables()
        nc.vector.tensor_copy(
            out=perm[:].rearrange("p (e j) -> p e j", e=2),
            in_=ident[:].rearrange("p (j e) -> p e j", e=2),
        )
        for pair in range(2):
            for g in range(PASSES):
                for r in (2 * pair, 2 * pair + 1):
                    cast_piece(0, r, g, "V" if r in (0,) else "S")
        pending = []
        late = []

        def turn_bank(th, g):
            kind, n = kinds[th // 2]
            bank(kind, n, th % 2, g)
            if kind == "k" and n + 1 < NQ:
                for i in range(2):
                    j = 2 * (4 * (th % 2) + g) + i
                    if j < 16:
                        cast_piece(n + 1, 2 * (j // 8) + j % 2, (j % 8) // 2, "S")

        for s in range(-3, 4 * NQ):
            th = s + 3
            if th == 2:
                for b in range(B):
                    do_x(b)
            for part in range(2):
                if s >= 0:
                    unit = units[2 * s + part]
                    multiply(*unit)
                    late.append(unit)

                if th < 4 * NQ:
                    for g in (2 * part, 2 * part + 1):
                        turn_bank(th, g)
                while late:
                    rope(*late.pop(0))
                for i in range(2):
                    if pending:
                        quant(*pending.pop(0))
            if th < 4 * NQ and th % 2 == 1:
                pending.extend([kinds[th // 2] + (g,) for g in range(PASSES)])
                while pending:
                    quant(*pending.pop(0))
        for unit in late:
            rope(*unit)
